import numpy as np
import ml_dtypes


def mxq(x, axis, fmt="e4m3"):
    dtype, down = {"e4m3": (ml_dtypes.float8_e4m3fn, 7), "e5m2": (ml_dtypes.float8_e5m2, 14)}[fmt]
    v = np.moveaxis(np.asarray(x, np.float32).astype(ml_dtypes.bfloat16).astype(np.float64), axis, -1)
    blocks = v.reshape(v.shape[:-1] + (-1, 32))
    amax = np.abs(blocks).max(-1, keepdims=True)
    byte = np.maximum(np.where(amax > 0, np.frexp(amax)[1] - 1 + 127, 0) - down, 1)
    scale = np.exp2(byte - 127.0)
    codes = (blocks / scale).astype(np.float32).astype(dtype).astype(np.float64)
    return np.moveaxis((codes * scale).reshape(v.shape), -1, axis)


WIDE = False


def mx_kscale(k):
    if not WIDE:
        return np.ones(k)
    levels = np.array([10, -10, 5, -5, 0])
    a = np.random.permutation(np.resize(levels, k // 512 * 4)).reshape(k // 512, 4)
    idx = np.arange(k)
    return np.exp2(a[idx // 512, idx % 128 // 32])


BF16 = ml_dtypes.bfloat16


def bf(x):
    return np.asarray(x, np.float32).astype(BF16)


def f64(x):
    return np.asarray(x).astype(np.float64)


NK, F, B = 12288, 512, 256
D = 2 * F
EPS = 1e-8


def rotate_half(x):
    d = x.shape[-1] // 2
    return np.concatenate([-x[..., d:], x[..., :d]], axis=-1)


def setup_inputs():
    sf = mx_kscale(F)
    s = np.concatenate([sf, sf])
    c = np.exp2(np.round(0.5 * np.log2(np.mean(1.0 / s**2))))
    return {"K": bf(np.random.standard_normal((NK, D)) * s * c),
            "reference_angles": bf(np.random.random(F) * 2.0 * np.pi),
            "probes": bf(np.random.standard_normal((B, D)) / s),
            "u_weights": bf(np.random.standard_normal((B, F)) * 0.5 / np.sqrt(F) / (sf * c)),
            "k_bias": bf(np.random.standard_normal(B) * 0.5)}


def reference(K, reference_angles, probes, u_weights, k_bias):
    K = f64(K)
    probes = f64(probes)
    pnorm = np.sqrt(np.sum(probes**2, axis=-1, keepdims=True))
    p = probes / (pnorm + EPS)
    theta_full = np.concatenate([f64(reference_angles), f64(reference_angles)], axis=-1)
    rotated = p * np.cos(theta_full) + rotate_half(p) * np.sin(theta_full)
    dot_term = mxq(K, 1, "e4m3") @ mxq(rotated, 1, "e4m3").T
    K_mag = np.sqrt(K[..., :F] ** 2 + K[..., F:] ** 2 + EPS)
    logits = dot_term + (mxq(K_mag, 1, "e4m3") @ mxq(f64(u_weights), 1, "e4m3").T) + f64(k_bias)
    return logits

@@ -1,0 +1,317 @@
+from contextlib import ExitStack
+
+import concourse.mybir as mybir
+from concourse.masks import make_identity
+
+F32 = mybir.dt.float32
+BF16 = mybir.dt.bfloat16
+U32 = mybir.dt.uint32
+U8 = mybir.dt.uint8
+FP8X4 = mybir.dt.float8_e4m3fn_x4
+ACT = mybir.ActivationFunctionType
+ALU = mybir.AluOpType
+
+N_KEYS, D, F, B = 12288, 1024, 512, 256
+EPS = 1e-8
+FLOPS = 2 * N_KEYS * B * (D + F)
+
+P = 128
+PACK = 4
+TILES = 2
+N_PAIRS = N_KEYS // (TILES * P)
+KEY_BUFS = 6
+
+TWO_PI_HI = 6.28125
+TWO_PI_MID = 0.0019353071693331003189
+TWO_PI_LO = 1.0253131677018245682e-11
+INV_TWO_PI = 0.15915493667125701904
+ROUND_MAGIC = 12582912.0
+PI_BELOW = 3.1415925025939941406
+
+
+def tile_module2network_t_kernel(tc, K, reference_angles, probes, u_weights, k_bias, out):
+    nc = tc.nc
+    with ExitStack() as ctx:
+        const = ctx.enter_context(tc.tile_pool(name="const", bufs=1))
+        setup = ctx.enter_context(tc.tile_pool(name="setup", bufs=1))
+        setup_tmp = ctx.enter_context(tc.tile_pool(name="setup_tmp", bufs=2))
+        key_pool = ctx.enter_context(tc.tile_pool(name="keys", bufs=KEY_BUFS))
+        square_pool = ctx.enter_context(tc.tile_pool(name="squares", bufs=3))
+        grouped_pool = ctx.enter_context(tc.tile_pool(name="grouped", bufs=3))
+        key_code_pool = ctx.enter_context(tc.tile_pool(name="key_codes", bufs=6))
+        mag_pool = ctx.enter_context(tc.tile_pool(name="mag", bufs=4))
+        mag_code_pool = ctx.enter_context(tc.tile_pool(name="mag_codes", bufs=6))
+        logit_pool = ctx.enter_context(tc.tile_pool(name="logits", bufs=4))
+        keyT_psum = ctx.enter_context(tc.psum_pool(name="keyT_psum", bufs=2))
+        sum_psum = ctx.enter_context(tc.psum_pool(name="sum_psum", bufs=4))
+        acc_psum = ctx.enter_context(tc.psum_pool(name="acc_psum", bufs=2))
+
+        K_pairs = K.rearrange("(j p t) d -> j p (t d)", p=P, t=TILES)
+        out_pairs = out.rearrange("(j p t) b -> j p (t b)", p=P, t=TILES)
+
+        angles = setup.tile([P, PACK], BF16)
+        nc.scalar.dma_start(
+            out=angles[:].rearrange("p (u e) -> p u e", e=2),
+            in_=reference_angles.rearrange("(u p e) -> p u e", u=2, e=2),
+        )
+        probes_sb = setup.tile([P, 2, D], BF16)
+        nc.scalar.dma_start(out=probes_sb[:], in_=probes.rearrange("(h p) d -> p h d", p=P))
+        u_sb = setup.tile([P, 2, F], BF16)
+        nc.scalar.dma_start(out=u_sb[:], in_=u_weights.rearrange("(h p) f -> p h f", p=P))
+        bias_rows = const.tile([P, B], BF16)
+        nc.scalar.dma_start(out=bias_rows[:], in_=k_bias.partition_broadcast(P))
+
+        ident_f32 = const.tile([P, P], F32)
+        make_identity(nc, ident_f32[:])
+        ident_bf16 = const.tile([P, P], BF16)
+        make_identity(nc, ident_bf16[:])
+        eps_col = const.tile([P, 1], F32)
+        nc.vector.memset(eps_col[:], EPS)
+
+        keys, keysT, squares, grouped = {}, {}, {}, {}
+        key_codes, sums, mags, mag_codes, accs = {}, {}, {}, {}, {}
+
+        def load_keys(j):
+            k_sb = key_pool.tile([P, TILES, D], BF16)
+            nc.sync.dma_start(out=k_sb[:].rearrange("p t d -> p (t d)"), in_=K_pairs[j])
+            keys[j] = k_sb
+
+        def transpose_keys(j):
+            words = keys[j][:].bitcast(F32)
+            banks = []
+            for t in range(TILES):
+                kT = keyT_psum.tile([P, PACK, P], F32)
+                for a in range(PACK):
+                    nc.tensor.transpose(kT[:, a, :], words[:, t, a * P : (a + 1) * P], ident_f32[:])
+                banks.append(kT)
+            keysT[j] = banks
+
+        def regroup_keys(j):
+            kg = grouped_pool.tile([P, 2, TILES, P, PACK], BF16, align_bytes=64)
+            kg_words = kg[:].bitcast(F32)
+            for t in range(TILES):
+                nc.vector.tensor_copy(
+                    out=kg_words[:, :, t, :, :],
+                    in_=keysT[j][t][:].rearrange("p (g u) n -> p g n u", u=2),
+                )
+            grouped[j] = kg
+
+        def quantise_keys(j):
+            kc = key_code_pool.tile([P, 2 * TILES * P], U32, align_bytes=64)
+            ks = key_code_pool.tile([P, 2 * TILES * P], U8, align_bytes=64)
+            nc.vector.quantize_mx(
+                out=kc[:].bitcast(FP8X4),
+                scales=ks[:],
+                in_=grouped[j][:].rearrange("p g t n k -> p (g t n k)"),
+            )
+            key_codes[j] = (kc, ks)
+
+        def square_keys(j):
+            sq = square_pool.tile([P, TILES, D], F32)
+            nc.scalar.activation(out=sq[:], in_=keys[j][:], func=ACT.Square)
+            squares[j] = sq
+
+        def add_squares(j):
+            banks = []
+            for t in range(TILES):
+                s_ps = sum_psum.tile([P, PACK, P], F32)
+                for k in range(PACK):
+                    for g in range(2):
+                        nc.tensor.matmul(
+                            out=s_ps[:, k, :],
+                            lhsT=squares[j][:, t, g * F + k * P : g * F + (k + 1) * P],
+                            rhs=ident_f32[:],
+                            is_transpose=True,
+                            start=(g == 0),
+                            stop=(g == 1),
+                        )
+                banks.append(s_ps)
+            sums[j] = banks
+
+        def root_magnitudes(j):
+            mg = mag_pool.tile([P, TILES, P, PACK], BF16, align_bytes=64)
+            for t in range(TILES):
+                nc.scalar.activation(
+                    out=mg[:, t, :, :],
+                    in_=sums[j][t][:].rearrange("p k n -> p n k"),
+                    func=ACT.Sqrt,
+                    bias=eps_col[:, 0:1],
+                )
+            mags[j] = mg
+
+        def quantise_magnitudes(j):
+            mc = mag_code_pool.tile([P, TILES * P], U32, align_bytes=64)
+            ms = mag_code_pool.tile([P, TILES * P], U8, align_bytes=64)
+            nc.vector.quantize_mx(
+                out=mc[:].bitcast(FP8X4),
+                scales=ms[:],
+                in_=mags[j][:].rearrange("p t n k -> p (t n k)"),
+            )
+            mag_codes[j] = (mc, ms)
+
+        def multiply(j):
+            kc, ks = key_codes[j]
+            mc, ms = mag_codes[j]
+            acc = acc_psum.tile([P, TILES, B], F32)
+            for t in range(TILES):
+                for g in range(2):
+                    key_cols = slice((g * TILES + t) * P, (g * TILES + t + 1) * P)
+                    nc.tensor.matmul_mx(
+                        out=acc[:, t, :],
+                        lhsT=kc[:, key_cols].bitcast(FP8X4),
+                        lhsT_scale=ks[:, key_cols],
+                        rhs=rot_codes[:, g * B : (g + 1) * B].bitcast(FP8X4),
+                        rhs_scale=rot_scales[:, g * B : (g + 1) * B],
+                        start=(g == 0),
+                        stop=False,
+                    )
+                nc.tensor.matmul_mx(
+                    out=acc[:, t, :],
+                    lhsT=mc[:, t * P : (t + 1) * P].bitcast(FP8X4),
+                    lhsT_scale=ms[:, t * P : (t + 1) * P],
+                    rhs=u_codes[:].bitcast(FP8X4),
+                    rhs_scale=u_scales[:],
+                    start=False,
+                    stop=True,
+                )
+            accs[j] = acc
+
+        def add_bias_and_store(j):
+            logits = logit_pool.tile([P, TILES, B], F32)
+            nc.vector.tensor_tensor(
+                out=logits[:],
+                in0=accs[j][:],
+                in1=bias_rows[:].unsqueeze(1).to_broadcast([P, TILES, B]),
+                op=ALU.add,
+            )
+            nc.sync.dma_start(out=out_pairs[j], in_=logits[:].rearrange("p t b -> p (t b)"))
+
+        def run(stage, j):
+            if 0 <= j < N_PAIRS:
+                stage(j)
+
+        for j in range(KEY_BUFS):
+            load_keys(j)
+
+        uT = acc_psum.tile([P, PACK, B], BF16, tag="acc")
+        for h in range(2):
+            for k in range(PACK):
+                nc.tensor.transpose(
+                    uT[:, k, h * P : (h + 1) * P], u_sb[:, h, k * P : (k + 1) * P], ident_bf16[:]
+                )
+        u_grouped = setup.tile([P, B, PACK], BF16, align_bytes=64)
+        nc.vector.tensor_copy(out=u_grouped[:], in_=uT[:].rearrange("p k b -> p b k"))
+        u_codes = const.tile([P, B], U32, align_bytes=64)
+        u_scales = const.tile([P, B], U8, align_bytes=64)
+        nc.vector.quantize_mx(
+            out=u_codes[:].bitcast(FP8X4),
+            scales=u_scales[:],
+            in_=u_grouped[:].rearrange("p b k -> p (b k)"),
+        )
+
+        shift = setup.tile([P, 2, PACK], F32)
+        nc.vector.memset(shift[:, 0, :], 0.0)
+        nc.vector.memset(shift[:, 1, :], 0.25)
+        theta = setup.tile([P, 2, PACK], F32)
+        nc.vector.tensor_copy(out=theta[:], in_=angles[:].unsqueeze(1).to_broadcast([P, 2, PACK]))
+        turns = setup.tile([P, 2, PACK], F32)
+        nc.vector.scalar_tensor_tensor(
+            out=turns[:], in0=theta[:], scalar=INV_TWO_PI, in1=shift[:], op0=ALU.mult, op1=ALU.add
+        )
+        whole = setup.tile([P, 2, PACK], F32)
+        nc.vector.tensor_scalar_add(out=whole[:], in0=turns[:], scalar1=ROUND_MAGIC)
+        q = setup.tile([P, 2, PACK], F32)
+        nc.vector.scalar_tensor_tensor(
+            out=q[:], in0=whole[:], scalar=ROUND_MAGIC, in1=shift[:], op0=ALU.subtract, op1=ALU.subtract
+        )
+        reduced_a = setup.tile([P, 2, PACK], F32)
+        nc.vector.scalar_tensor_tensor(
+            out=reduced_a[:], in0=q[:], scalar=-TWO_PI_HI, in1=theta[:], op0=ALU.mult, op1=ALU.add
+        )
+        reduced_b = setup.tile([P, 2, PACK], F32)
+        nc.vector.scalar_tensor_tensor(
+            out=reduced_b[:], in0=q[:], scalar=-TWO_PI_MID, in1=reduced_a[:], op0=ALU.mult, op1=ALU.add
+        )
+        reduced_c = setup.tile([P, 2, PACK], F32)
+        nc.vector.scalar_tensor_tensor(
+            out=reduced_c[:], in0=q[:], scalar=-TWO_PI_LO, in1=reduced_b[:], op0=ALU.mult, op1=ALU.add
+        )
+        reduced = setup.tile([P, 2, PACK], F32)
+        nc.vector.tensor_scalar(
+            out=reduced[:], in0=reduced_c[:], scalar1=PI_BELOW, scalar2=-PI_BELOW, op0=ALU.min, op1=ALU.max
+        )
+        sin_cos = setup.tile([P, 2, PACK], F32)
+        nc.scalar.activation(out=sin_cos[:], in_=reduced[:], func=ACT.Sin)
+
+        squared_probes = setup.tile([P, 2, D], BF16)
+        norm_sq = setup.tile([P, 2], F32)
+        for h in range(2):
+            nc.scalar.activation(
+                out=squared_probes[:, h, :],
+                in_=probes_sb[:, h, :],
+                func=ACT.Square,
+                accum_out=norm_sq[:, h : h + 1],
+            )
+        norm = setup.tile([P, 2], F32)
+        nc.scalar.activation(out=norm[:], in_=norm_sq[:], func=ACT.Sqrt)
+        norm_eps = setup.tile([P, 2], F32)
+        nc.vector.tensor_scalar_add(out=norm_eps[:], in0=norm[:], scalar1=EPS)
+        inv_norm = setup.tile([P, 2], F32)
+        nc.vector.reciprocal(out=inv_norm[:], in_=norm_eps[:])
+        unit = setup.tile([P, 2, D], F32)
+        for h in range(2):
+            nc.vector.tensor_scalar_mul(
+                out=unit[:, h, :], in0=probes_sb[:, h, :], scalar1=inv_norm[:, h : h + 1]
+            )
+        unit_blocks = unit[:].rearrange("b h (a p e) -> b h a e p", a=PACK, e=2)
+        planes = setup.tile([P, 2, PACK, B], BF16)
+        for u in range(2):
+            re_ps = acc_psum.tile([P, 2, B], F32, tag="acc")
+            im_ps = acc_psum.tile([P, 2, B], F32, tag="acc")
+            for e in range(2):
+                for h in range(2):
+                    nc.tensor.transpose(
+                        re_ps[:, e, h * P : (h + 1) * P], unit_blocks[:, h, u, e, :], ident_f32[:]
+                    )
+                    nc.tensor.transpose(
+                        im_ps[:, e, h * P : (h + 1) * P], unit_blocks[:, h, 2 + u, e, :], ident_f32[:]
+                    )
+            for e in range(2):
+                c = 2 * u + e
+                sin_col = sin_cos[:, 0, c : c + 1]
+                cos_col = sin_cos[:, 1, c : c + 1]
+                im_sin = setup_tmp.tile([P, B], F32)
+                nc.vector.tensor_scalar_mul(out=im_sin[:], in0=im_ps[:, e, :], scalar1=sin_col)
+                nc.vector.scalar_tensor_tensor(
+                    out=planes[:, 0, c, :], in0=re_ps[:, e, :], scalar=cos_col, in1=im_sin[:],
+                    op0=ALU.mult, op1=ALU.subtract,
+                )
+                re_sin = setup_tmp.tile([P, B], F32)
+                nc.vector.tensor_scalar_mul(out=re_sin[:], in0=re_ps[:, e, :], scalar1=sin_col)
+                nc.vector.scalar_tensor_tensor(
+                    out=planes[:, 1, c, :], in0=im_ps[:, e, :], scalar=cos_col, in1=re_sin[:],
+                    op0=ALU.mult, op1=ALU.add,
+                )
+        rot_grouped = setup.tile([P, 2, B, PACK], BF16, align_bytes=64)
+        nc.vector.tensor_copy(out=rot_grouped[:], in_=planes[:].rearrange("p g k b -> p g b k"))
+        rot_codes = const.tile([P, 2 * B], U32, align_bytes=64)
+        rot_scales = const.tile([P, 2 * B], U8, align_bytes=64)
+        nc.vector.quantize_mx(
+            out=rot_codes[:].bitcast(FP8X4),
+            scales=rot_scales[:],
+            in_=rot_grouped[:].rearrange("p g b k -> p (g b k)"),
+        )
+
+        transpose_keys(0)
+        square_keys(0)
+        for step in range(N_PAIRS + 3):
+            run(regroup_keys, step)
+            run(transpose_keys, step + 1)
+            run(square_keys, step + 1)
+            run(load_keys, step + KEY_BUFS)
+            run(quantise_magnitudes, step - 2)
+            run(multiply, step - 2)
+            run(quantise_keys, step)
+            run(add_squares, step)
+            run(root_magnitudes, step - 1)
+            run(add_bias_and_store, step - 3)

@@ -20,6 +20,7 @@ PACK = 4
 TILES = 2
 N_PAIRS = N_KEYS // (TILES * P)
 KEY_BUFS = 6
+GPSIMD_SQUARES = TILES * D // 4
 
 TWO_PI_HI = 6.28125
 TWO_PI_MID = 0.0019353071693331003189
@@ -108,7 +109,13 @@ def tile_module2network_t_kernel(tc, K, reference_angles, probes, u_weights, k_b
 
         def square_keys(j):
             sq = square_pool.tile([P, TILES, D], F32)
-            nc.scalar.activation(out=sq[:], in_=keys[j][:], func=ACT.Square)
+            sq_flat = sq[:].rearrange("p t d -> p (t d)")
+            k_flat = keys[j][:].rearrange("p t d -> p (t d)")
+            cut = TILES * D - GPSIMD_SQUARES
+            nc.scalar.activation(out=sq_flat[:, 0:cut], in_=k_flat[:, 0:cut], func=ACT.Square)
+            nc.gpsimd.tensor_tensor(
+                out=sq_flat[:, cut:], in0=k_flat[:, cut:], in1=k_flat[:, cut:], op=ALU.mult
+            )
             squares[j] = sq
 
         def add_squares(j):

@@ -20,7 +20,7 @@ PACK = 4
 TILES = 2
 N_PAIRS = N_KEYS // (TILES * P)
 KEY_BUFS = 6
-GPSIMD_SQUARES = TILES * D // 4
+VECTOR_SQUARES = TILES * D // 8
 
 TWO_PI_HI = 6.28125
 TWO_PI_MID = 0.0019353071693331003189
@@ -111,9 +111,9 @@ def tile_module2network_t_kernel(tc, K, reference_angles, probes, u_weights, k_b
             sq = square_pool.tile([P, TILES, D], F32)
             sq_flat = sq[:].rearrange("p t d -> p (t d)")
             k_flat = keys[j][:].rearrange("p t d -> p (t d)")
-            cut = TILES * D - GPSIMD_SQUARES
+            cut = TILES * D - VECTOR_SQUARES
             nc.scalar.activation(out=sq_flat[:, 0:cut], in_=k_flat[:, 0:cut], func=ACT.Square)
-            nc.gpsimd.tensor_tensor(
+            nc.vector.tensor_tensor(
                 out=sq_flat[:, cut:], in0=k_flat[:, cut:], in1=k_flat[:, cut:], op=ALU.mult
             )
             squares[j] = sq
@@ -309,16 +309,17 @@ def tile_module2network_t_kernel(tc, K, reference_angles, probes, u_weights, k_b
             in_=rot_grouped[:].rearrange("p g b k -> p (g b k)"),
         )
 
-        transpose_keys(0)
-        square_keys(0)
-        for step in range(N_PAIRS + 3):
-            run(regroup_keys, step)
-            run(transpose_keys, step + 1)
-            run(square_keys, step + 1)
-            run(load_keys, step + KEY_BUFS)
-            run(quantise_magnitudes, step - 2)
-            run(multiply, step - 2)
-            run(quantise_keys, step)
-            run(add_squares, step)
-            run(root_magnitudes, step - 1)
-            run(add_bias_and_store, step - 3)
+        with tc.manual_schedule():
+            transpose_keys(0)
+            square_keys(0)
+            for step in range(N_PAIRS + 4):
+                run(regroup_keys, step)
+                run(transpose_keys, step + 1)
+                run(square_keys, step + 1)
+                run(load_keys, step + KEY_BUFS)
+                run(quantise_magnitudes, step - 2)
+                run(multiply, step - 3)
+                run(quantise_keys, step)
+                run(add_squares, step)
+                run(root_magnitudes, step - 1)
+                run(add_bias_and_store, step - 4)

@@ -118,19 +118,29 @@ def tile_module2network_t_kernel(tc, K, reference_angles, probes, u_weights, k_b
             )
             squares[j] = sq
 
-        def add_squares(j):
+        def add_odd_tiles(j):
+            for t in range(1, TILES, 2):
+                nc.gpsimd.tensor_tensor(
+                    out=squares[j][:, t, 0:F],
+                    in0=squares[j][:, t, 0:F],
+                    in1=squares[j][:, t, F:D],
+                    op=ALU.add,
+                )
+
+        def transpose_sums(j):
             banks = []
             for t in range(TILES):
+                terms = 2 if t % 2 == 0 else 1
                 s_ps = sum_psum.tile([P, PACK, P], F32)
                 for k in range(PACK):
-                    for g in range(2):
+                    for g in range(terms):
                         nc.tensor.matmul(
                             out=s_ps[:, k, :],
                             lhsT=squares[j][:, t, g * F + k * P : g * F + (k + 1) * P],
                             rhs=ident_f32[:],
                             is_transpose=True,
                             start=(g == 0),
-                            stop=(g == 1),
+                            stop=(g == terms - 1),
                         )
                 banks.append(s_ps)
             sums[j] = banks
@@ -313,6 +323,7 @@ def tile_module2network_t_kernel(tc, K, reference_angles, probes, u_weights, k_b
             transpose_keys(0)
             square_keys(0)
             for step in range(N_PAIRS + 4):
+                run(add_odd_tiles, step)
                 run(regroup_keys, step)
                 run(transpose_keys, step + 1)
                 run(square_keys, step + 1)
@@ -320,6 +331,6 @@ def tile_module2network_t_kernel(tc, K, reference_angles, probes, u_weights, k_b
                 run(quantise_magnitudes, step - 2)
                 run(multiply, step - 3)
                 run(quantise_keys, step)
-                run(add_squares, step)
+                run(transpose_sums, step)
                 run(root_magnitudes, step - 1)
                 run(add_bias_and_store, step - 4)

@@ -20,7 +20,7 @@ PACK = 4
 TILES = 2
 N_PAIRS = N_KEYS // (TILES * P)
 KEY_BUFS = 6
-VECTOR_SQUARES = TILES * D // 8
+MX_LAG = 5
 
 TWO_PI_HI = 6.28125
 TWO_PI_MID = 0.0019353071693331003189
@@ -39,7 +39,7 @@ def tile_module2network_t_kernel(tc, K, reference_angles, probes, u_weights, k_b
         key_pool = ctx.enter_context(tc.tile_pool(name="keys", bufs=KEY_BUFS))
         square_pool = ctx.enter_context(tc.tile_pool(name="squares", bufs=3))
         grouped_pool = ctx.enter_context(tc.tile_pool(name="grouped", bufs=3))
-        key_code_pool = ctx.enter_context(tc.tile_pool(name="key_codes", bufs=6))
+        key_code_pool = ctx.enter_context(tc.tile_pool(name="key_codes", bufs=MX_LAG + 3))
         mag_pool = ctx.enter_context(tc.tile_pool(name="mag", bufs=4))
         mag_code_pool = ctx.enter_context(tc.tile_pool(name="mag_codes", bufs=6))
         logit_pool = ctx.enter_context(tc.tile_pool(name="logits", bufs=4))
@@ -111,21 +111,16 @@ def tile_module2network_t_kernel(tc, K, reference_angles, probes, u_weights, k_b
             sq = square_pool.tile([P, TILES, D], F32)
             sq_flat = sq[:].rearrange("p t d -> p (t d)")
             k_flat = keys[j][:].rearrange("p t d -> p (t d)")
-            cut = TILES * D - VECTOR_SQUARES
-            nc.scalar.activation(out=sq_flat[:, 0:cut], in_=k_flat[:, 0:cut], func=ACT.Square)
-            nc.vector.tensor_tensor(
-                out=sq_flat[:, cut:], in0=k_flat[:, cut:], in1=k_flat[:, cut:], op=ALU.mult
+            nc.scalar.activation(out=sq_flat[:, 0 : D + F], in_=k_flat[:, 0 : D + F], func=ACT.Square)
+            nc.gpsimd.tensor_tensor(
+                out=sq[:, 1, F:D], in0=keys[j][:, 1, F:D], in1=keys[j][:, 1, F:D], op=ALU.mult
             )
             squares[j] = sq
 
-        def add_odd_tiles(j):
-            for t in range(1, TILES, 2):
-                nc.gpsimd.tensor_tensor(
-                    out=squares[j][:, t, 0:F],
-                    in0=squares[j][:, t, 0:F],
-                    in1=squares[j][:, t, F:D],
-                    op=ALU.add,
-                )
+        def add_odd_tile(j):
+            nc.gpsimd.tensor_tensor(
+                out=squares[j][:, 1, 0:F], in0=squares[j][:, 1, 0:F], in1=squares[j][:, 1, F:D], op=ALU.add
+            )
 
         def transpose_sums(j):
             banks = []
@@ -322,15 +317,15 @@ def tile_module2network_t_kernel(tc, K, reference_angles, probes, u_weights, k_b
         with tc.manual_schedule():
             transpose_keys(0)
             square_keys(0)
-            for step in range(N_PAIRS + 4):
-                run(add_odd_tiles, step)
+            for step in range(N_PAIRS + MX_LAG + 1):
+                run(add_odd_tile, step)
                 run(regroup_keys, step)
                 run(transpose_keys, step + 1)
                 run(square_keys, step + 1)
                 run(load_keys, step + KEY_BUFS)
                 run(quantise_magnitudes, step - 2)
-                run(multiply, step - 3)
+                run(multiply, step - MX_LAG)
                 run(quantise_keys, step)
                 run(transpose_sums, step)
                 run(root_magnitudes, step - 1)
-                run(add_bias_and_store, step - 4)
+                run(add_bias_and_store, step - MX_LAG - 1)

@@ -20,6 +20,7 @@ PACK = 4
 TILES = 2
 N_PAIRS = N_KEYS // (TILES * P)
 KEY_BUFS = 6
+VECTOR_SQUARES = TILES * D // 8
 MX_LAG = 5
 
 TWO_PI_HI = 6.28125
@@ -77,15 +78,12 @@ def tile_module2network_t_kernel(tc, K, reference_angles, probes, u_weights, k_b
             nc.sync.dma_start(out=k_sb[:].rearrange("p t d -> p (t d)"), in_=K_pairs[j])
             keys[j] = k_sb
 
-        def transpose_keys(j):
+        def transpose_keys(j, t):
             words = keys[j][:].bitcast(F32)
-            banks = []
-            for t in range(TILES):
-                kT = keyT_psum.tile([P, PACK, P], F32)
-                for a in range(PACK):
-                    nc.tensor.transpose(kT[:, a, :], words[:, t, a * P : (a + 1) * P], ident_f32[:])
-                banks.append(kT)
-            keysT[j] = banks
+            kT = keyT_psum.tile([P, PACK, P], F32)
+            for a in range(PACK):
+                nc.tensor.transpose(kT[:, a, :], words[:, t, a * P : (a + 1) * P], ident_f32[:])
+            keysT[(j, t)] = kT
 
         def regroup_keys(j):
             kg = grouped_pool.tile([P, 2, TILES, P, PACK], BF16, align_bytes=64)
@@ -93,7 +91,7 @@ def tile_module2network_t_kernel(tc, K, reference_angles, probes, u_weights, k_b
             for t in range(TILES):
                 nc.vector.tensor_copy(
                     out=kg_words[:, :, t, :, :],
-                    in_=keysT[j][t][:].rearrange("p (g u) n -> p g n u", u=2),
+                    in_=keysT[(j, t)][:].rearrange("p (g u) n -> p g n u", u=2),
                 )
             grouped[j] = kg
 
@@ -111,41 +109,43 @@ def tile_module2network_t_kernel(tc, K, reference_angles, probes, u_weights, k_b
             sq = square_pool.tile([P, TILES, D], F32)
             sq_flat = sq[:].rearrange("p t d -> p (t d)")
             k_flat = keys[j][:].rearrange("p t d -> p (t d)")
-            nc.scalar.activation(out=sq_flat[:, 0 : D + F], in_=k_flat[:, 0 : D + F], func=ACT.Square)
-            nc.gpsimd.tensor_tensor(
-                out=sq[:, 1, F:D], in0=keys[j][:, 1, F:D], in1=keys[j][:, 1, F:D], op=ALU.mult
+            cut = TILES * D - VECTOR_SQUARES
+            nc.scalar.activation(out=sq_flat[:, 0:cut], in_=k_flat[:, 0:cut], func=ACT.Square)
+            nc.vector.tensor_tensor(
+                out=sq_flat[:, cut:], in0=k_flat[:, cut:], in1=k_flat[:, cut:], op=ALU.mult
             )
             squares[j] = sq
 
-        def add_odd_tile(j):
-            nc.gpsimd.tensor_tensor(
-                out=squares[j][:, 1, 0:F], in0=squares[j][:, 1, 0:F], in1=squares[j][:, 1, F:D], op=ALU.add
-            )
+        def add_odd_tiles(j):
+            for t in range(1, TILES, 2):
+                nc.gpsimd.tensor_tensor(
+                    out=squares[j][:, t, 0:F],
+                    in0=squares[j][:, t, 0:F],
+                    in1=squares[j][:, t, F:D],
+                    op=ALU.add,
+                )
 
-        def transpose_sums(j):
-            banks = []
-            for t in range(TILES):
-                terms = 2 if t % 2 == 0 else 1
-                s_ps = sum_psum.tile([P, PACK, P], F32)
-                for k in range(PACK):
-                    for g in range(terms):
-                        nc.tensor.matmul(
-                            out=s_ps[:, k, :],
-                            lhsT=squares[j][:, t, g * F + k * P : g * F + (k + 1) * P],
-                            rhs=ident_f32[:],
-                            is_transpose=True,
-                            start=(g == 0),
-                            stop=(g == terms - 1),
-                        )
-                banks.append(s_ps)
-            sums[j] = banks
+        def transpose_sums(j, t):
+            terms = 2 if t % 2 == 0 else 1
+            s_ps = sum_psum.tile([P, PACK, P], F32)
+            for k in range(PACK):
+                for g in range(terms):
+                    nc.tensor.matmul(
+                        out=s_ps[:, k, :],
+                        lhsT=squares[j][:, t, g * F + k * P : g * F + (k + 1) * P],
+                        rhs=ident_f32[:],
+                        is_transpose=True,
+                        start=(g == 0),
+                        stop=(g == terms - 1),
+                    )
+            sums[(j, t)] = s_ps
 
         def root_magnitudes(j):
             mg = mag_pool.tile([P, TILES, P, PACK], BF16, align_bytes=64)
             for t in range(TILES):
                 nc.scalar.activation(
                     out=mg[:, t, :, :],
-                    in_=sums[j][t][:].rearrange("p k n -> p n k"),
+                    in_=sums[(j, t)][:].rearrange("p k n -> p n k"),
                     func=ACT.Sqrt,
                     bias=eps_col[:, 0:1],
                 )
@@ -161,32 +161,32 @@ def tile_module2network_t_kernel(tc, K, reference_angles, probes, u_weights, k_b
             )
             mag_codes[j] = (mc, ms)
 
-        def multiply(j):
+        def multiply(j, t):
             kc, ks = key_codes[j]
             mc, ms = mag_codes[j]
-            acc = acc_psum.tile([P, TILES, B], F32)
-            for t in range(TILES):
-                for g in range(2):
-                    key_cols = slice((g * TILES + t) * P, (g * TILES + t + 1) * P)
-                    nc.tensor.matmul_mx(
-                        out=acc[:, t, :],
-                        lhsT=kc[:, key_cols].bitcast(FP8X4),
-                        lhsT_scale=ks[:, key_cols],
-                        rhs=rot_codes[:, g * B : (g + 1) * B].bitcast(FP8X4),
-                        rhs_scale=rot_scales[:, g * B : (g + 1) * B],
-                        start=(g == 0),
-                        stop=False,
-                    )
+            if t == 0:
+                acc = acc_psum.tile([P, TILES, B], F32)
+                accs[j] = acc
+            for g in range(2):
+                key_cols = slice((g * TILES + t) * P, (g * TILES + t + 1) * P)
                 nc.tensor.matmul_mx(
-                    out=acc[:, t, :],
-                    lhsT=mc[:, t * P : (t + 1) * P].bitcast(FP8X4),
-                    lhsT_scale=ms[:, t * P : (t + 1) * P],
-                    rhs=u_codes[:].bitcast(FP8X4),
-                    rhs_scale=u_scales[:],
-                    start=False,
-                    stop=True,
+                    out=accs[j][:, t, :],
+                    lhsT=kc[:, key_cols].bitcast(FP8X4),
+                    lhsT_scale=ks[:, key_cols],
+                    rhs=rot_codes[:, g * B : (g + 1) * B].bitcast(FP8X4),
+                    rhs_scale=rot_scales[:, g * B : (g + 1) * B],
+                    start=(g == 0),
+                    stop=False,
                 )
-            accs[j] = acc
+            nc.tensor.matmul_mx(
+                out=accs[j][:, t, :],
+                lhsT=mc[:, t * P : (t + 1) * P].bitcast(FP8X4),
+                lhsT_scale=ms[:, t * P : (t + 1) * P],
+                rhs=u_codes[:].bitcast(FP8X4),
+                rhs_scale=u_scales[:],
+                start=False,
+                stop=True,
+            )
 
         def add_bias_and_store(j):
             logits = logit_pool.tile([P, TILES, B], F32)
@@ -198,9 +198,9 @@ def tile_module2network_t_kernel(tc, K, reference_angles, probes, u_weights, k_b
             )
             nc.sync.dma_start(out=out_pairs[j], in_=logits[:].rearrange("p t b -> p (t b)"))
 
-        def run(stage, j):
+        def run(stage, j, *tile_index):
             if 0 <= j < N_PAIRS:
-                stage(j)
+                stage(j, *tile_index)
 
         for j in range(KEY_BUFS):
             load_keys(j)
@@ -315,17 +315,19 @@ def tile_module2network_t_kernel(tc, K, reference_angles, probes, u_weights, k_b
         )
 
         with tc.manual_schedule():
-            transpose_keys(0)
+            for t in range(TILES):
+                transpose_keys(0, t)
             square_keys(0)
             for step in range(N_PAIRS + MX_LAG + 1):
-                run(add_odd_tile, step)
+                run(add_odd_tiles, step)
                 run(regroup_keys, step)
-                run(transpose_keys, step + 1)
                 run(square_keys, step + 1)
                 run(load_keys, step + KEY_BUFS)
                 run(quantise_magnitudes, step - 2)
-                run(multiply, step - MX_LAG)
+                for t in range(TILES):
+                    run(transpose_keys, step + 1, t)
+                    run(transpose_sums, step, t)
+                    run(multiply, step - MX_LAG, t)
                 run(quantise_keys, step)
-                run(transpose_sums, step)
                 run(root_magnitudes, step - 1)
                 run(add_bias_and_store, step - MX_LAG - 1)

from contextlib import ExitStack

import concourse.mybir as mybir
from concourse.masks import make_identity

F32 = mybir.dt.float32
BF16 = mybir.dt.bfloat16
U32 = mybir.dt.uint32
U8 = mybir.dt.uint8
FP8X4 = mybir.dt.float8_e4m3fn_x4
ACT = mybir.ActivationFunctionType
ALU = mybir.AluOpType

N_KEYS, D, F, B = 12288, 1024, 512, 256
EPS = 1e-8
FLOPS = 2 * N_KEYS * B * (D + F)

P = 128
PACK = 4
TILES = 2
N_PAIRS = N_KEYS // (TILES * P)
KEY_BUFS = 6
VECTOR_SQUARES = TILES * D // 8
MX_LAG = 5

TWO_PI_HI = 6.28125
TWO_PI_MID = 0.0019353071693331003189
TWO_PI_LO = 1.0253131677018245682e-11
INV_TWO_PI = 0.15915493667125701904
ROUND_MAGIC = 12582912.0
PI_BELOW = 3.1415925025939941406


def tile_module2network_t_kernel(tc, K, reference_angles, probes, u_weights, k_bias, out):
    nc = tc.nc
    with ExitStack() as ctx:
        const = ctx.enter_context(tc.tile_pool(name="const", bufs=1))
        setup = ctx.enter_context(tc.tile_pool(name="setup", bufs=1))
        setup_tmp = ctx.enter_context(tc.tile_pool(name="setup_tmp", bufs=2))
        key_pool = ctx.enter_context(tc.tile_pool(name="keys", bufs=KEY_BUFS))
        square_pool = ctx.enter_context(tc.tile_pool(name="squares", bufs=3))
        grouped_pool = ctx.enter_context(tc.tile_pool(name="grouped", bufs=3))
        key_code_pool = ctx.enter_context(tc.tile_pool(name="key_codes", bufs=MX_LAG + 3))
        mag_pool = ctx.enter_context(tc.tile_pool(name="mag", bufs=4))
        mag_code_pool = ctx.enter_context(tc.tile_pool(name="mag_codes", bufs=6))
        logit_pool = ctx.enter_context(tc.tile_pool(name="logits", bufs=4))
        keyT_psum = ctx.enter_context(tc.psum_pool(name="keyT_psum", bufs=2))
        sum_psum = ctx.enter_context(tc.psum_pool(name="sum_psum", bufs=4))
        acc_psum = ctx.enter_context(tc.psum_pool(name="acc_psum", bufs=2))

        K_pairs = K.rearrange("(j p t) d -> j p (t d)", p=P, t=TILES)
        out_pairs = out.rearrange("(j p t) b -> j p (t b)", p=P, t=TILES)

        angles = setup.tile([P, PACK], BF16)
        nc.scalar.dma_start(
            out=angles[:].rearrange("p (u e) -> p u e", e=2),
            in_=reference_angles.rearrange("(u p e) -> p u e", u=2, e=2),
        )
        probes_sb = setup.tile([P, 2, D], BF16)
        nc.scalar.dma_start(out=probes_sb[:], in_=probes.rearrange("(h p) d -> p h d", p=P))
        u_sb = setup.tile([P, 2, F], BF16)
        nc.scalar.dma_start(out=u_sb[:], in_=u_weights.rearrange("(h p) f -> p h f", p=P))
        bias_rows = const.tile([P, B], BF16)
        nc.scalar.dma_start(out=bias_rows[:], in_=k_bias.partition_broadcast(P))

        ident_f32 = const.tile([P, P], F32)
        make_identity(nc, ident_f32[:])
        ident_bf16 = const.tile([P, P], BF16)
        make_identity(nc, ident_bf16[:])
        eps_col = const.tile([P, 1], F32)
        nc.vector.memset(eps_col[:], EPS)

        keys, keysT, squares, grouped = {}, {}, {}, {}
        key_codes, sums, mags, mag_codes, accs = {}, {}, {}, {}, {}

        def load_keys(j):
            k_sb = key_pool.tile([P, TILES, D], BF16)
            nc.sync.dma_start(out=k_sb[:].rearrange("p t d -> p (t d)"), in_=K_pairs[j])
            keys[j] = k_sb

        def transpose_keys(j, t):
            words = keys[j][:].bitcast(F32)
            kT = keyT_psum.tile([P, PACK, P], F32)
            for a in range(PACK):
                nc.tensor.transpose(kT[:, a, :], words[:, t, a * P : (a + 1) * P], ident_f32[:])
            keysT[(j, t)] = kT

        def regroup_keys(j):
            kg = grouped_pool.tile([P, 2, TILES, P, PACK], BF16, align_bytes=64)
            kg_words = kg[:].bitcast(F32)
            for t in range(TILES):
                nc.vector.tensor_copy(
                    out=kg_words[:, :, t, :, :],
                    in_=keysT[(j, t)][:].rearrange("p (g u) n -> p g n u", u=2),
                )
            grouped[j] = kg

        def quantise_keys(j):
            kc = key_code_pool.tile([P, 2 * TILES * P], U32, align_bytes=64)
            ks = key_code_pool.tile([P, 2 * TILES * P], U8, align_bytes=64)
            nc.vector.quantize_mx(
                out=kc[:].bitcast(FP8X4),
                scales=ks[:],
                in_=grouped[j][:].rearrange("p g t n k -> p (g t n k)"),
            )
            key_codes[j] = (kc, ks)

        def square_keys(j):
            sq = square_pool.tile([P, TILES, D], F32)
            sq_flat = sq[:].rearrange("p t d -> p (t d)")
            k_flat = keys[j][:].rearrange("p t d -> p (t d)")
            cut = TILES * D - VECTOR_SQUARES
            nc.scalar.activation(out=sq_flat[:, 0:cut], in_=k_flat[:, 0:cut], func=ACT.Square)
            nc.vector.tensor_tensor(
                out=sq_flat[:, cut:], in0=k_flat[:, cut:], in1=k_flat[:, cut:], op=ALU.mult
            )
            squares[j] = sq

        def add_odd_tiles(j):
            for t in range(1, TILES, 2):
                nc.gpsimd.tensor_tensor(
                    out=squares[j][:, t, 0:F],
                    in0=squares[j][:, t, 0:F],
                    in1=squares[j][:, t, F:D],
                    op=ALU.add,
                )

        def transpose_sums(j, t):
            terms = 2 if t % 2 == 0 else 1
            s_ps = sum_psum.tile([P, PACK, P], F32)
            for k in range(PACK):
                for g in range(terms):
                    nc.tensor.matmul(
                        out=s_ps[:, k, :],
                        lhsT=squares[j][:, t, g * F + k * P : g * F + (k + 1) * P],
                        rhs=ident_f32[:],
                        is_transpose=True,
                        start=(g == 0),
                        stop=(g == terms - 1),
                    )
            sums[(j, t)] = s_ps

        def root_magnitudes(j):
            mg = mag_pool.tile([P, TILES, P, PACK], BF16, align_bytes=64)
            for t in range(TILES):
                nc.scalar.activation(
                    out=mg[:, t, :, :],
                    in_=sums[(j, t)][:].rearrange("p k n -> p n k"),
                    func=ACT.Sqrt,
                    bias=eps_col[:, 0:1],
                )
            mags[j] = mg

        def quantise_magnitudes(j):
            mc = mag_code_pool.tile([P, TILES * P], U32, align_bytes=64)
            ms = mag_code_pool.tile([P, TILES * P], U8, align_bytes=64)
            nc.vector.quantize_mx(
                out=mc[:].bitcast(FP8X4),
                scales=ms[:],
                in_=mags[j][:].rearrange("p t n k -> p (t n k)"),
            )
            mag_codes[j] = (mc, ms)

        def multiply(j, t):
            kc, ks = key_codes[j]
            mc, ms = mag_codes[j]
            if t == 0:
                acc = acc_psum.tile([P, TILES, B], F32)
                accs[j] = acc
            for g in range(2):
                key_cols = slice((g * TILES + t) * P, (g * TILES + t + 1) * P)
                nc.tensor.matmul_mx(
                    out=accs[j][:, t, :],
                    lhsT=kc[:, key_cols].bitcast(FP8X4),
                    lhsT_scale=ks[:, key_cols],
                    rhs=rot_codes[:, g * B : (g + 1) * B].bitcast(FP8X4),
                    rhs_scale=rot_scales[:, g * B : (g + 1) * B],
                    start=(g == 0),
                    stop=False,
                )
            nc.tensor.matmul_mx(
                out=accs[j][:, t, :],
                lhsT=mc[:, t * P : (t + 1) * P].bitcast(FP8X4),
                lhsT_scale=ms[:, t * P : (t + 1) * P],
                rhs=u_codes[:].bitcast(FP8X4),
                rhs_scale=u_scales[:],
                start=False,
                stop=True,
            )

        def add_bias_and_store(j):
            logits = logit_pool.tile([P, TILES, B], F32)
            nc.vector.tensor_tensor(
                out=logits[:],
                in0=accs[j][:],
                in1=bias_rows[:].unsqueeze(1).to_broadcast([P, TILES, B]),
                op=ALU.add,
            )
            nc.sync.dma_start(out=out_pairs[j], in_=logits[:].rearrange("p t b -> p (t b)"))

        def run(stage, j, *tile_index):
            if 0 <= j < N_PAIRS:
                stage(j, *tile_index)

        for j in range(KEY_BUFS):
            load_keys(j)

        uT = acc_psum.tile([P, PACK, B], BF16, tag="acc")
        for h in range(2):
            for k in range(PACK):
                nc.tensor.transpose(
                    uT[:, k, h * P : (h + 1) * P], u_sb[:, h, k * P : (k + 1) * P], ident_bf16[:]
                )
        u_grouped = setup.tile([P, B, PACK], BF16, align_bytes=64)
        nc.vector.tensor_copy(out=u_grouped[:], in_=uT[:].rearrange("p k b -> p b k"))
        u_codes = const.tile([P, B], U32, align_bytes=64)
        u_scales = const.tile([P, B], U8, align_bytes=64)
        nc.vector.quantize_mx(
            out=u_codes[:].bitcast(FP8X4),
            scales=u_scales[:],
            in_=u_grouped[:].rearrange("p b k -> p (b k)"),
        )

        shift = setup.tile([P, 2, PACK], F32)
        nc.vector.memset(shift[:, 0, :], 0.0)
        nc.vector.memset(shift[:, 1, :], 0.25)
        theta = setup.tile([P, 2, PACK], F32)
        nc.vector.tensor_copy(out=theta[:], in_=angles[:].unsqueeze(1).to_broadcast([P, 2, PACK]))
        turns = setup.tile([P, 2, PACK], F32)
        nc.vector.scalar_tensor_tensor(
            out=turns[:], in0=theta[:], scalar=INV_TWO_PI, in1=shift[:], op0=ALU.mult, op1=ALU.add
        )
        whole = setup.tile([P, 2, PACK], F32)
        nc.vector.tensor_scalar_add(out=whole[:], in0=turns[:], scalar1=ROUND_MAGIC)
        q = setup.tile([P, 2, PACK], F32)
        nc.vector.scalar_tensor_tensor(
            out=q[:], in0=whole[:], scalar=ROUND_MAGIC, in1=shift[:], op0=ALU.subtract, op1=ALU.subtract
        )
        reduced_a = setup.tile([P, 2, PACK], F32)
        nc.vector.scalar_tensor_tensor(
            out=reduced_a[:], in0=q[:], scalar=-TWO_PI_HI, in1=theta[:], op0=ALU.mult, op1=ALU.add
        )
        reduced_b = setup.tile([P, 2, PACK], F32)
        nc.vector.scalar_tensor_tensor(
            out=reduced_b[:], in0=q[:], scalar=-TWO_PI_MID, in1=reduced_a[:], op0=ALU.mult, op1=ALU.add
        )
        reduced_c = setup.tile([P, 2, PACK], F32)
        nc.vector.scalar_tensor_tensor(
            out=reduced_c[:], in0=q[:], scalar=-TWO_PI_LO, in1=reduced_b[:], op0=ALU.mult, op1=ALU.add
        )
        reduced = setup.tile([P, 2, PACK], F32)
        nc.vector.tensor_scalar(
            out=reduced[:], in0=reduced_c[:], scalar1=PI_BELOW, scalar2=-PI_BELOW, op0=ALU.min, op1=ALU.max
        )
        sin_cos = setup.tile([P, 2, PACK], F32)
        nc.scalar.activation(out=sin_cos[:], in_=reduced[:], func=ACT.Sin)

        squared_probes = setup.tile([P, 2, D], BF16)
        norm_sq = setup.tile([P, 2], F32)
        for h in range(2):
            nc.scalar.activation(
                out=squared_probes[:, h, :],
                in_=probes_sb[:, h, :],
                func=ACT.Square,
                accum_out=norm_sq[:, h : h + 1],
            )
        norm = setup.tile([P, 2], F32)
        nc.scalar.activation(out=norm[:], in_=norm_sq[:], func=ACT.Sqrt)
        norm_eps = setup.tile([P, 2], F32)
        nc.vector.tensor_scalar_add(out=norm_eps[:], in0=norm[:], scalar1=EPS)
        inv_norm = setup.tile([P, 2], F32)
        nc.vector.reciprocal(out=inv_norm[:], in_=norm_eps[:])
        unit = setup.tile([P, 2, D], F32)
        for h in range(2):
            nc.vector.tensor_scalar_mul(
                out=unit[:, h, :], in0=probes_sb[:, h, :], scalar1=inv_norm[:, h : h + 1]
            )
        unit_blocks = unit[:].rearrange("b h (a p e) -> b h a e p", a=PACK, e=2)
        planes = setup.tile([P, 2, PACK, B], BF16)
        for u in range(2):
            re_ps = acc_psum.tile([P, 2, B], F32, tag="acc")
            im_ps = acc_psum.tile([P, 2, B], F32, tag="acc")
            for e in range(2):
                for h in range(2):
                    nc.tensor.transpose(
                        re_ps[:, e, h * P : (h + 1) * P], unit_blocks[:, h, u, e, :], ident_f32[:]
                    )
                    nc.tensor.transpose(
                        im_ps[:, e, h * P : (h + 1) * P], unit_blocks[:, h, 2 + u, e, :], ident_f32[:]
                    )
            for e in range(2):
                c = 2 * u + e
                sin_col = sin_cos[:, 0, c : c + 1]
                cos_col = sin_cos[:, 1, c : c + 1]
                im_sin = setup_tmp.tile([P, B], F32)
                nc.vector.tensor_scalar_mul(out=im_sin[:], in0=im_ps[:, e, :], scalar1=sin_col)
                nc.vector.scalar_tensor_tensor(
                    out=planes[:, 0, c, :], in0=re_ps[:, e, :], scalar=cos_col, in1=im_sin[:],
                    op0=ALU.mult, op1=ALU.subtract,
                )
                re_sin = setup_tmp.tile([P, B], F32)
                nc.vector.tensor_scalar_mul(out=re_sin[:], in0=re_ps[:, e, :], scalar1=sin_col)
                nc.vector.scalar_tensor_tensor(
                    out=planes[:, 1, c, :], in0=im_ps[:, e, :], scalar=cos_col, in1=re_sin[:],
                    op0=ALU.mult, op1=ALU.add,
                )
        rot_grouped = setup.tile([P, 2, B, PACK], BF16, align_bytes=64)
        nc.vector.tensor_copy(out=rot_grouped[:], in_=planes[:].rearrange("p g k b -> p g b k"))
        rot_codes = const.tile([P, 2 * B], U32, align_bytes=64)
        rot_scales = const.tile([P, 2 * B], U8, align_bytes=64)
        nc.vector.quantize_mx(
            out=rot_codes[:].bitcast(FP8X4),
            scales=rot_scales[:],
            in_=rot_grouped[:].rearrange("p g b k -> p (g b k)"),
        )

        with tc.manual_schedule():
            for t in range(TILES):
                transpose_keys(0, t)
            square_keys(0)
            for step in range(N_PAIRS + MX_LAG + 1):
                run(add_odd_tiles, step)
                run(regroup_keys, step)
                run(square_keys, step + 1)
                run(load_keys, step + KEY_BUFS)
                run(quantise_magnitudes, step - 2)
                for t in range(TILES):
                    run(transpose_keys, step + 1, t)
                    run(transpose_sums, step, t)
                    run(multiply, step - MX_LAG, t)
                run(quantise_keys, step)
                run(root_magnitudes, step - 1)
                run(add_bias_and_store, step - MX_LAG - 1)
